import numpy as np
import ml_dtypes

BF16 = ml_dtypes.bfloat16


def bf(x):
    return np.asarray(x, np.float32).astype(BF16)


def f32(x):
    return np.asarray(x, np.float32)


def f64(x):
    return np.asarray(x).astype(np.float64)


def striped(idx):
    return np.tile(idx.reshape(-1, 16).T, (8, 1))


C, S, N = 256, 2048, 1024


def sigmoid(v):
    return 1.0 / (1.0 + np.exp(-v))


def setup_inputs():
    return {"x": bf(np.random.standard_normal((C, N)) + np.random.standard_normal((C, 1))), "adj_t": f32(np.random.standard_normal((C, C)) / np.sqrt(C)), "para": f32(np.random.standard_normal((C, N))), "base": f32(np.random.standard_normal((C, S))), "offs": striped(np.random.permutation(S)[:N])}


def reference(x, adj_t, para, base, offs):
    idx = offs[:16].T.reshape(-1)
    xv = f64(x)
    m = xv.mean(axis=1)
    s = 2.0 * np.abs(np.abs(sigmoid(m[:, None] - m[None, :]) - 0.5) - 0.5)
    a_t = f64(adj_t) * s
    y = a_t.T @ xv
    p = f64(para)
    out = f64(base).copy()
    out[:, idx] = np.maximum(y * np.sign(p), 0.0) * np.abs(p)
    return out

@@ -1,0 +1,92 @@
+import concourse.mybir as mybir
+from concourse.masks import make_identity
+
+P = 128
+C, S, N = 256, 2048, 1024
+BLOCKS = C // P
+PIECE = 512
+PIECES = N // PIECE
+FLOPS = 2 * C * C * N
+
+F32, BF16, U16 = mybir.dt.float32, mybir.dt.bfloat16, mybir.dt.uint16
+FUNC = mybir.ActivationFunctionType
+ALU = mybir.AluOpType
+
+
+def tile_tce_kernel(tc, x, adj_t, para, base, offs, out):
+    nc = tc.nc
+    with (
+        tc.tile_pool(name="held", bufs=1) as held,
+        tc.tile_pool(name="work", bufs=2) as work,
+        tc.tile_pool(name="pieces", bufs=4) as pieces,
+        tc.psum_pool(name="psum_row", bufs=1) as psum_row,
+        tc.psum_pool(name="psum_y", bufs=4) as psum_y,
+    ):
+        offsets = held.tile([P, N // 16], U16, name="offsets")
+        x_sb = [held.tile([P, N], BF16, name=f"x_sb{b}") for b in range(BLOCKS)]
+        adj_sb = [held.tile([P, C], F32, name=f"adj_sb{b}") for b in range(BLOCKS)]
+        para_sb = [held.tile([P, N], F32, name=f"para_sb{b}") for b in range(BLOCKS)]
+        window = [held.tile([P, S], F32, name=f"window{b}") for b in range(BLOCKS)]
+
+        nc.sync.dma_start(x_sb[0][:], x[0:P, :])
+        nc.scalar.dma_start(x_sb[1][:], x[P : 2 * P, :])
+        nc.sync.dma_start(adj_sb[0][:], adj_t[0:P, :])
+        nc.scalar.dma_start(adj_sb[1][:], adj_t[P : 2 * P, :])
+        nc.sync.dma_start(offsets[:], offs)
+        nc.sync.dma_start(para_sb[0][:], para[0:P, :])
+        nc.scalar.dma_start(para_sb[1][:], para[P : 2 * P, :])
+
+        identity = held.tile([P, P], F32, name="identity")
+        make_identity(nc, identity[:])
+        for b in range(BLOCKS):
+            nc.gpsimd.dma_start(window[b][:], base[b * P : (b + 1) * P, :])
+
+        rowsum = [held.tile([P, 1], F32, name=f"rowsum{b}") for b in range(BLOCKS)]
+        nc.vector.reduce_sum(rowsum[0][:], x_sb[0][:], axis=mybir.AxisListType.X)
+        copied = held.tile([P, N], BF16, name="copied")
+        nc.scalar.activation(copied[:], x_sb[1][:], FUNC.Copy, accum_out=rowsum[1][:])
+
+        sums_row = psum_row.tile([P, C], F32, name="sums_row")
+        for b in range(BLOCKS):
+            repeated = work.tile([P, P], F32, name="repeated")
+            nc.vector.tensor_copy(repeated[:], rowsum[b][:, 0:1].to_broadcast([P, P]))
+            nc.tensor.transpose(sums_row[:, b * P : (b + 1) * P], repeated[:], identity[:])
+
+        mix = [held.tile([P, C], BF16, name=f"mix{k}") for k in range(BLOCKS)]
+        for k in range(BLOCKS):
+            gap = work.tile([P, C], F32, name="gap")
+            nc.scalar.activation(gap[:], sums_row[:], FUNC.Abs, bias=rowsum[k][:, 0:1], scale=-1.0)
+            half_s = work.tile([P, C], F32, name="half_s")
+            nc.scalar.activation(half_s[:], gap[:], FUNC.Sigmoid, scale=-1.0 / N)
+            nc.vector.scalar_tensor_tensor(
+                mix[k][:], half_s[:], 2.0, adj_sb[k][:], op0=ALU.mult, op1=ALU.mult
+            )
+
+        for c in range(BLOCKS):
+            for h in range(PIECES):
+                cols = slice(h * PIECE, (h + 1) * PIECE)
+                sgn = pieces.tile([P, PIECE], F32, name="sgn")
+                nc.scalar.activation(sgn[:], para_sb[c][:, cols], FUNC.Sign)
+                mag = pieces.tile([P, PIECE], F32, name="mag")
+                nc.scalar.activation(mag[:], para_sb[c][:, cols], FUNC.Abs)
+
+                y = psum_y.tile([P, PIECE], F32, name="y")
+                for k in range(BLOCKS):
+                    nc.tensor.matmul(
+                        y[:],
+                        mix[k][:, c * P : (c + 1) * P],
+                        x_sb[k][:, cols],
+                        start=(k == 0),
+                        stop=(k == BLOCKS - 1),
+                    )
+                signed = pieces.tile([P, PIECE], F32, name="signed")
+                nc.vector.tensor_tensor(signed[:], y[:], sgn[:], ALU.mult)
+                rectified = pieces.tile([P, PIECE], F32, name="rectified")
+                nc.scalar.activation(rectified[:], signed[:], FUNC.Relu)
+                nc.vector.tensor_tensor(
+                    window[c][:].indirect(offsets[:, h * (PIECE // 16) : (h + 1) * (PIECE // 16)]),
+                    rectified[:],
+                    mag[:],
+                    ALU.mult,
+                )
+            nc.sync.dma_start(out[c * P : (c + 1) * P, :], window[c][:])

@@ -18,39 +18,43 @@ def tile_tce_kernel(tc, x, adj_t, para, base, offs, out):
     with (
         tc.tile_pool(name="held", bufs=1) as held,
         tc.tile_pool(name="work", bufs=2) as work,
-        tc.tile_pool(name="pieces", bufs=4) as pieces,
+        tc.tile_pool(name="pieces", bufs=2) as pieces,
         tc.psum_pool(name="psum_row", bufs=1) as psum_row,
         tc.psum_pool(name="psum_y", bufs=4) as psum_y,
     ):
         offsets = held.tile([P, N // 16], U16, name="offsets")
-        x_sb = [held.tile([P, N], BF16, name=f"x_sb{b}") for b in range(BLOCKS)]
-        adj_sb = [held.tile([P, C], F32, name=f"adj_sb{b}") for b in range(BLOCKS)]
+        x_sb = held.tile([P, BLOCKS, N], BF16, name="x_sb")
+        adj_sb = held.tile([P, BLOCKS, C], F32, name="adj_sb")
         para_sb = [held.tile([P, N], F32, name=f"para_sb{b}") for b in range(BLOCKS)]
         window = [held.tile([P, S], F32, name=f"window{b}") for b in range(BLOCKS)]
 
-        nc.sync.dma_start(x_sb[0][:], x[0:P, :])
-        nc.scalar.dma_start(x_sb[1][:], x[P : 2 * P, :])
-        nc.sync.dma_start(adj_sb[0][:], adj_t[0:P, :])
-        nc.scalar.dma_start(adj_sb[1][:], adj_t[P : 2 * P, :])
-        nc.sync.dma_start(offsets[:], offs)
+        nc.sync.dma_start(x_sb[:, 0, :], x[0:P, :])
+        nc.scalar.dma_start(x_sb[:, 1, :], x[P : 2 * P, :])
         nc.sync.dma_start(para_sb[0][:], para[0:P, :])
-        nc.scalar.dma_start(para_sb[1][:], para[P : 2 * P, :])
+        nc.sync.dma_start(para_sb[1][:], para[P : 2 * P, :])
+        nc.sync.dma_start(adj_sb[:], adj_t.rearrange("(b p) c -> p b c", p=P))
+        nc.sync.dma_start(offsets[:], offs)
+        nc.sync.dma_start(window[0][:], base[0:P, :])
+        nc.sync.dma_start(window[1][:], base[P : 2 * P, :])
 
         identity = held.tile([P, P], F32, name="identity")
         make_identity(nc, identity[:])
-        for b in range(BLOCKS):
-            nc.gpsimd.dma_start(window[b][:], base[b * P : (b + 1) * P, :])
+
+        warm = held.tile([P, 1], F32, name="warm")
+        nc.vector.memset(warm[:], 0.0)
+        warmed = held.tile([P, 1], F32, name="warmed")
+        nc.scalar.activation(warmed[:], warm[:], FUNC.Sigmoid)
 
         rowsum = [held.tile([P, 1], F32, name=f"rowsum{b}") for b in range(BLOCKS)]
-        nc.vector.reduce_sum(rowsum[0][:], x_sb[0][:], axis=mybir.AxisListType.X)
+        nc.vector.reduce_sum(rowsum[0][:], x_sb[:, 0, :], axis=mybir.AxisListType.X)
         copied = held.tile([P, N], BF16, name="copied")
-        nc.scalar.activation(copied[:], x_sb[1][:], FUNC.Copy, accum_out=rowsum[1][:])
+        nc.scalar.activation(copied[:], x_sb[:, 1, :], FUNC.Copy, accum_out=rowsum[1][:])
 
         sums_row = psum_row.tile([P, C], F32, name="sums_row")
         for b in range(BLOCKS):
-            repeated = work.tile([P, P], F32, name="repeated")
-            nc.vector.tensor_copy(repeated[:], rowsum[b][:, 0:1].to_broadcast([P, P]))
-            nc.tensor.transpose(sums_row[:, b * P : (b + 1) * P], repeated[:], identity[:])
+            nc.tensor.transpose(
+                sums_row[:, b * P : (b + 1) * P], rowsum[b][:, 0:1].to_broadcast([P, P]), identity[:]
+            )
 
         mix = [held.tile([P, C], BF16, name=f"mix{k}") for k in range(BLOCKS)]
         for k in range(BLOCKS):
@@ -59,34 +63,45 @@ def tile_tce_kernel(tc, x, adj_t, para, base, offs, out):
             half_s = work.tile([P, C], F32, name="half_s")
             nc.scalar.activation(half_s[:], gap[:], FUNC.Sigmoid, scale=-1.0 / N)
             nc.vector.scalar_tensor_tensor(
-                mix[k][:], half_s[:], 2.0, adj_sb[k][:], op0=ALU.mult, op1=ALU.mult
+                mix[k][:], half_s[:], 2.0, adj_sb[:, k, :], op0=ALU.mult, op1=ALU.mult
             )
 
+        mag = [held.tile([P, N], F32, name=f"mag{c}") for c in range(BLOCKS)]
         for c in range(BLOCKS):
-            for h in range(PIECES):
-                cols = slice(h * PIECE, (h + 1) * PIECE)
-                sgn = pieces.tile([P, PIECE], F32, name="sgn")
-                nc.scalar.activation(sgn[:], para_sb[c][:, cols], FUNC.Sign)
-                mag = pieces.tile([P, PIECE], F32, name="mag")
-                nc.scalar.activation(mag[:], para_sb[c][:, cols], FUNC.Abs)
+            nc.vector.scalar_tensor_tensor(
+                mag[c][:], para_sb[c][:], -1.0, para_sb[c][:], op0=ALU.mult, op1=ALU.max
+            )
 
-                y = psum_y.tile([P, PIECE], F32, name="y")
-                for k in range(BLOCKS):
-                    nc.tensor.matmul(
-                        y[:],
-                        mix[k][:, c * P : (c + 1) * P],
-                        x_sb[k][:, cols],
-                        start=(k == 0),
-                        stop=(k == BLOCKS - 1),
-                    )
-                signed = pieces.tile([P, PIECE], F32, name="signed")
-                nc.vector.tensor_tensor(signed[:], y[:], sgn[:], ALU.mult)
-                rectified = pieces.tile([P, PIECE], F32, name="rectified")
-                nc.scalar.activation(rectified[:], signed[:], FUNC.Relu)
-                nc.vector.tensor_tensor(
-                    window[c][:].indirect(offsets[:, h * (PIECE // 16) : (h + 1) * (PIECE // 16)]),
-                    rectified[:],
-                    mag[:],
-                    ALU.mult,
+        def prepare(c, h):
+            cols = slice(h * PIECE, (h + 1) * PIECE)
+            sgn = pieces.tile([P, PIECE], F32, name="sgn")
+            nc.scalar.activation(sgn[:], para_sb[c][:, cols], FUNC.Sign)
+            y = psum_y.tile([P, PIECE], F32, name="y")
+            for k in range(BLOCKS):
+                nc.tensor.matmul(
+                    y[:],
+                    mix[k][:, c * P : (c + 1) * P],
+                    x_sb[:, k, cols],
+                    start=(k == 0),
+                    stop=(k == BLOCKS - 1),
                 )
-            nc.sync.dma_start(out[c * P : (c + 1) * P, :], window[c][:])
+            signed = pieces.tile([P, PIECE], F32, name="signed")
+            nc.vector.tensor_tensor(signed[:], y[:], sgn[:], ALU.mult)
+            rectified = pieces.tile([P, PIECE], F32, name="rectified")
+            nc.scalar.activation(rectified[:], signed[:], FUNC.Relu)
+            return rectified
+
+        order = [(c, h) for c in range(BLOCKS) for h in range(PIECES)]
+        prepared = prepare(*order[0])
+        for i, (c, h) in enumerate(order):
+            rectified = prepared
+            if i + 1 < len(order):
+                prepared = prepare(*order[i + 1])
+            nc.vector.tensor_tensor(
+                window[c][:].indirect(offsets[:, h * (PIECE // 16) : (h + 1) * (PIECE // 16)]),
+                rectified[:],
+                mag[c][:, h * PIECE : (h + 1) * PIECE],
+                ALU.mult,
+            )
+            if h == PIECES - 1:
+                nc.sync.dma_start(out[c * P : (c + 1) * P, :], window[c][:])

@@ -7,6 +7,7 @@ BLOCKS = C // P
 PIECE = 512
 PIECES = N // PIECE
 FLOPS = 2 * C * C * N
+WARM_UPS = 8
 
 F32, BF16, U16 = mybir.dt.float32, mybir.dt.bfloat16, mybir.dt.uint16
 FUNC = mybir.ActivationFunctionType
@@ -39,6 +40,10 @@ def tile_tce_kernel(tc, x, adj_t, para, base, offs, out):
 
         identity = held.tile([P, P], F32, name="identity")
         make_identity(nc, identity[:])
+
+        idle_work = psum_row.tile([P, P], F32, name="idle_work")
+        for i in range(WARM_UPS):
+            nc.tensor.matmul(idle_work[:], identity[:], identity[:], start=True, stop=True)
 
         warm = held.tile([P, 1], F32, name="warm")
         nc.vector.memset(warm[:], 0.0)

@@ -18,10 +18,11 @@ def tile_tce_kernel(tc, x, adj_t, para, base, offs, out):
     nc = tc.nc
     with (
         tc.tile_pool(name="held", bufs=1) as held,
-        tc.tile_pool(name="work", bufs=2) as work,
-        tc.tile_pool(name="pieces", bufs=2) as pieces,
+        tc.tile_pool(name="work", bufs=BLOCKS) as work,
+        tc.tile_pool(name="ring", bufs=BLOCKS * PIECES) as ring,
+        tc.tile_pool(name="pieces", bufs=BLOCKS * PIECES) as pieces,
         tc.psum_pool(name="psum_row", bufs=1) as psum_row,
-        tc.psum_pool(name="psum_y", bufs=4) as psum_y,
+        tc.psum_pool(name="psum_y", bufs=BLOCKS * PIECES) as psum_y,
     ):
         offsets = held.tile([P, N // 16], U16, name="offsets")
         x_sb = held.tile([P, BLOCKS, N], BF16, name="x_sb")
@@ -65,7 +66,7 @@ def tile_tce_kernel(tc, x, adj_t, para, base, offs, out):
         for k in range(BLOCKS):
             gap = work.tile([P, C], F32, name="gap")
             nc.scalar.activation(gap[:], sums_row[:], FUNC.Abs, bias=rowsum[k][:, 0:1], scale=-1.0)
-            half_s = work.tile([P, C], F32, name="half_s")
+            half_s = ring.tile([P, C], F32, name="half_s", tag="scalar_out")
             nc.scalar.activation(half_s[:], gap[:], FUNC.Sigmoid, scale=-1.0 / N)
             nc.vector.scalar_tensor_tensor(
                 mix[k][:], half_s[:], 2.0, adj_sb[:, k, :], op0=ALU.mult, op1=ALU.mult
@@ -77,9 +78,12 @@ def tile_tce_kernel(tc, x, adj_t, para, base, offs, out):
                 mag[c][:], para_sb[c][:], -1.0, para_sb[c][:], op0=ALU.mult, op1=ALU.max
             )
 
-        def prepare(c, h):
+        order = [(c, h) for c in range(BLOCKS) for h in range(PIECES)]
+
+        rectified = []
+        for c, h in order:
             cols = slice(h * PIECE, (h + 1) * PIECE)
-            sgn = pieces.tile([P, PIECE], F32, name="sgn")
+            sgn = ring.tile([P, PIECE], F32, name="sgn", tag="scalar_out")
             nc.scalar.activation(sgn[:], para_sb[c][:, cols], FUNC.Sign)
             y = psum_y.tile([P, PIECE], F32, name="y")
             for k in range(BLOCKS):
@@ -92,19 +96,13 @@ def tile_tce_kernel(tc, x, adj_t, para, base, offs, out):
                 )
             signed = pieces.tile([P, PIECE], F32, name="signed")
             nc.vector.tensor_tensor(signed[:], y[:], sgn[:], ALU.mult)
-            rectified = pieces.tile([P, PIECE], F32, name="rectified")
-            nc.scalar.activation(rectified[:], signed[:], FUNC.Relu)
-            return rectified
+            rectified.append(pieces.tile([P, PIECE], F32, name="rectified"))
+            nc.scalar.activation(rectified[-1][:], signed[:], FUNC.Relu)
 
-        order = [(c, h) for c in range(BLOCKS) for h in range(PIECES)]
-        prepared = prepare(*order[0])
         for i, (c, h) in enumerate(order):
-            rectified = prepared
-            if i + 1 < len(order):
-                prepared = prepare(*order[i + 1])
             nc.vector.tensor_tensor(
                 window[c][:].indirect(offsets[:, h * (PIECE // 16) : (h + 1) * (PIECE // 16)]),
-                rectified[:],
+                rectified[i][:],
                 mag[c][:, h * PIECE : (h + 1) * PIECE],
                 ALU.mult,
             )

@@ -7,7 +7,8 @@ BLOCKS = C // P
 PIECE = 512
 PIECES = N // PIECE
 FLOPS = 2 * C * C * N
-WARM_UPS = 8
+WARM_UPS = 4
+KEEP_WARM = 2
 
 F32, BF16, U16 = mybir.dt.float32, mybir.dt.bfloat16, mybir.dt.uint16
 FUNC = mybir.ActivationFunctionType
@@ -19,7 +20,7 @@ def tile_tce_kernel(tc, x, adj_t, para, base, offs, out):
     with (
         tc.tile_pool(name="held", bufs=1) as held,
         tc.tile_pool(name="work", bufs=BLOCKS) as work,
-        tc.tile_pool(name="ring", bufs=BLOCKS * PIECES) as ring,
+        tc.tile_pool(name="ring", bufs=2 * BLOCKS) as ring,
         tc.tile_pool(name="pieces", bufs=BLOCKS * PIECES) as pieces,
         tc.psum_pool(name="psum_row", bufs=1) as psum_row,
         tc.psum_pool(name="psum_y", bufs=BLOCKS * PIECES) as psum_y,
@@ -33,8 +34,8 @@ def tile_tce_kernel(tc, x, adj_t, para, base, offs, out):
         nc.sync.dma_start(x_sb[:, 0, :], x[0:P, :])
         nc.scalar.dma_start(x_sb[:, 1, :], x[P : 2 * P, :])
         nc.sync.dma_start(para_sb[0][:], para[0:P, :])
-        nc.sync.dma_start(para_sb[1][:], para[P : 2 * P, :])
         nc.sync.dma_start(adj_sb[:], adj_t.rearrange("(b p) c -> p b c", p=P))
+        nc.sync.dma_start(para_sb[1][:], para[P : 2 * P, :])
         nc.sync.dma_start(offsets[:], offs)
         nc.sync.dma_start(window[0][:], base[0:P, :])
         nc.sync.dma_start(window[1][:], base[P : 2 * P, :])
@@ -52,59 +53,77 @@ def tile_tce_kernel(tc, x, adj_t, para, base, offs, out):
         nc.scalar.activation(warmed[:], warm[:], FUNC.Sigmoid)
 
         rowsum = [held.tile([P, 1], F32, name=f"rowsum{b}") for b in range(BLOCKS)]
-        nc.vector.reduce_sum(rowsum[0][:], x_sb[:, 0, :], axis=mybir.AxisListType.X)
-        copied = held.tile([P, N], BF16, name="copied")
-        nc.scalar.activation(copied[:], x_sb[:, 1, :], FUNC.Copy, accum_out=rowsum[1][:])
-
-        sums_row = psum_row.tile([P, C], F32, name="sums_row")
         for b in range(BLOCKS):
-            nc.tensor.transpose(
-                sums_row[:, b * P : (b + 1) * P], rowsum[b][:, 0:1].to_broadcast([P, P]), identity[:]
+            copied = work.tile([P, N], BF16, name="copied")
+            nc.vector.tensor_scalar(
+                copied[:], x_sb[:, b, :], 1.0, None, op0=ALU.mult, op1=ALU.add, accum_out=rowsum[b][:]
             )
 
-        mix = [held.tile([P, C], BF16, name=f"mix{k}") for k in range(BLOCKS)]
-        for k in range(BLOCKS):
-            gap = work.tile([P, C], F32, name="gap")
-            nc.scalar.activation(gap[:], sums_row[:], FUNC.Abs, bias=rowsum[k][:, 0:1], scale=-1.0)
-            half_s = ring.tile([P, C], F32, name="half_s", tag="scalar_out")
-            nc.scalar.activation(half_s[:], gap[:], FUNC.Sigmoid, scale=-1.0 / N)
-            nc.vector.scalar_tensor_tensor(
-                mix[k][:], half_s[:], 2.0, adj_sb[:, k, :], op0=ALU.mult, op1=ALU.mult
+        sums_row = [psum_row.tile([P, P], F32, name=f"sums_row{b}") for b in range(BLOCKS)]
+        for b in range(BLOCKS):
+            nc.tensor.transpose(sums_row[b][:], rowsum[b][:, 0:1].to_broadcast([P, P]), identity[:])
+
+        for i in range(KEEP_WARM):
+            nc.tensor.matmul(
+                idle_work[:], identity[:], rowsum[BLOCKS - 1][:, 0:1].to_broadcast([P, P]), start=True, stop=True
             )
 
-        mag = [held.tile([P, N], F32, name=f"mag{c}") for c in range(BLOCKS)]
+        def cols(h):
+            return slice(h * PIECE, (h + 1) * PIECE)
+
+        twice_pos = held.tile([P, N], F32, name="twice_pos")
+        nc.vector.tensor_scalar(twice_pos[:], para_sb[0][:], 0.0, 2.0, op0=ALU.is_ge, op1=ALU.mult)
+
+        def weight_tile(c, name):
+            if c == 0:
+                return work.tile([P, P], F32, name=name)
+            return ring.tile([P, P], F32, name=name, tag="scalar_out")
+
+        mix = {}
         for c in range(BLOCKS):
-            nc.vector.scalar_tensor_tensor(
-                mag[c][:], para_sb[c][:], -1.0, para_sb[c][:], op0=ALU.mult, op1=ALU.max
-            )
-
-        order = [(c, h) for c in range(BLOCKS) for h in range(PIECES)]
-
-        rectified = []
-        for c, h in order:
-            cols = slice(h * PIECE, (h + 1) * PIECE)
-            sgn = ring.tile([P, PIECE], F32, name="sgn", tag="scalar_out")
-            nc.scalar.activation(sgn[:], para_sb[c][:, cols], FUNC.Sign)
-            y = psum_y.tile([P, PIECE], F32, name="y")
+            gap = [weight_tile(c, "gap") for k in range(BLOCKS)]
             for k in range(BLOCKS):
-                nc.tensor.matmul(
-                    y[:],
-                    mix[k][:, c * P : (c + 1) * P],
-                    x_sb[:, k, cols],
-                    start=(k == 0),
-                    stop=(k == BLOCKS - 1),
+                nc.scalar.activation(gap[k][:], sums_row[c][:], FUNC.Abs, bias=rowsum[k][:, 0:1], scale=-1.0)
+            half_s = [weight_tile(c, "half_s") for k in range(BLOCKS)]
+            for k in range(BLOCKS):
+                nc.scalar.activation(half_s[k][:], gap[k][:], FUNC.Sigmoid, scale=-1.0 / N)
+            for k in range(BLOCKS):
+                mix[c, k] = held.tile([P, P], BF16, name=f"mix{c}{k}")
+                nc.vector.scalar_tensor_tensor(
+                    mix[c, k][:], half_s[k][:], 2.0, adj_sb[:, k, c * P : (c + 1) * P], op0=ALU.mult, op1=ALU.mult
                 )
-            signed = pieces.tile([P, PIECE], F32, name="signed")
-            nc.vector.tensor_tensor(signed[:], y[:], sgn[:], ALU.mult)
-            rectified.append(pieces.tile([P, PIECE], F32, name="rectified"))
-            nc.scalar.activation(rectified[-1][:], signed[:], FUNC.Relu)
 
-        for i, (c, h) in enumerate(order):
-            nc.vector.tensor_tensor(
-                window[c][:].indirect(offsets[:, h * (PIECE // 16) : (h + 1) * (PIECE // 16)]),
-                rectified[i][:],
-                mag[c][:, h * PIECE : (h + 1) * PIECE],
-                ALU.mult,
-            )
-            if h == PIECES - 1:
-                nc.sync.dma_start(out[c * P : (c + 1) * P, :], window[c][:])
+        sgn = []
+        for h in range(PIECES):
+            sgn.append(ring.tile([P, PIECE], F32, name="sgn", tag="scalar_out"))
+            nc.scalar.activation(sgn[h][:], para_sb[1][:, cols(h)], FUNC.Sign)
+
+        rectified, mag = {}, {}
+        for c in range(BLOCKS):
+            for h in range(PIECES):
+                y = psum_y.tile([P, PIECE], F32, name="y")
+                for k in range(BLOCKS):
+                    nc.tensor.matmul(
+                        y[:], mix[c, k][:], x_sb[:, k, cols(h)], start=(k == 0), stop=(k == BLOCKS - 1)
+                    )
+                signed = pieces.tile([P, PIECE], F32, name="signed")
+                if c == 0:
+                    nc.vector.scalar_tensor_tensor(
+                        signed[:], twice_pos[:, cols(h)], -1.0, y[:], op0=ALU.add, op1=ALU.mult
+                    )
+                else:
+                    nc.vector.tensor_tensor(signed[:], y[:], sgn[h][:], ALU.mult)
+                rectified[c, h] = pieces.tile([P, PIECE], F32, name="rectified")
+                nc.scalar.activation(rectified[c, h][:], signed[:], FUNC.Relu)
+                mag[c, h] = ring.tile([P, PIECE], F32, name="mag", tag="scalar_out")
+                nc.scalar.activation(mag[c, h][:], para_sb[c][:, cols(h)], FUNC.Abs)
+
+        for c in range(BLOCKS):
+            for h in range(PIECES):
+                nc.vector.tensor_tensor(
+                    window[c][:].indirect(offsets[:, h * (PIECE // 16) : (h + 1) * (PIECE // 16)]),
+                    rectified[c, h][:],
+                    mag[c, h][:],
+                    ALU.mult,
+                )
+            nc.sync.dma_start(out[c * P : (c + 1) * P, :], window[c][:])

@@ -74,17 +74,12 @@ def tile_tce_kernel(tc, x, adj_t, para, base, offs, out):
         twice_pos = held.tile([P, N], F32, name="twice_pos")
         nc.vector.tensor_scalar(twice_pos[:], para_sb[0][:], 0.0, 2.0, op0=ALU.is_ge, op1=ALU.mult)
 
-        def weight_tile(c, name):
-            if c == 0:
-                return work.tile([P, P], F32, name=name)
-            return ring.tile([P, P], F32, name=name, tag="scalar_out")
-
         mix = {}
         for c in range(BLOCKS):
-            gap = [weight_tile(c, "gap") for k in range(BLOCKS)]
+            gap = [work.tile([P, P], F32, name="gap") for k in range(BLOCKS)]
             for k in range(BLOCKS):
                 nc.scalar.activation(gap[k][:], sums_row[c][:], FUNC.Abs, bias=rowsum[k][:, 0:1], scale=-1.0)
-            half_s = [weight_tile(c, "half_s") for k in range(BLOCKS)]
+            half_s = [ring.tile([P, P], F32, name="half_s", tag="scalar_out") for k in range(BLOCKS)]
             for k in range(BLOCKS):
                 nc.scalar.activation(half_s[k][:], gap[k][:], FUNC.Sigmoid, scale=-1.0 / N)
             for k in range(BLOCKS):

@@ -6,6 +6,7 @@ C, S, N = 256, 2048, 1024
 BLOCKS = C // P
 PIECE = 512
 PIECES = N // PIECE
+STORES = 4
 FLOPS = 2 * C * C * N
 WARM_UPS = 4
 KEEP_WARM = 2
@@ -121,4 +122,7 @@ def tile_tce_kernel(tc, x, adj_t, para, base, offs, out):
                     mag[c, h][:],
                     ALU.mult,
                 )
-            nc.sync.dma_start(out[c * P : (c + 1) * P, :], window[c][:])
+            for q in range(STORES):
+                queue = nc.sync if q % 2 == 0 else nc.scalar
+                run = slice(q * (S // STORES), (q + 1) * (S // STORES))
+                queue.dma_start(out[c * P : (c + 1) * P, run], window[c][:, run])

@@ -123,6 +123,5 @@ def tile_tce_kernel(tc, x, adj_t, para, base, offs, out):
                     ALU.mult,
                 )
             for q in range(STORES):
-                queue = nc.sync if q % 2 == 0 else nc.scalar
                 run = slice(q * (S // STORES), (q + 1) * (S // STORES))
-                queue.dma_start(out[c * P : (c + 1) * P, run], window[c][:, run])
+                nc.sync.dma_start(out[c * P : (c + 1) * P, run], window[c][:, run])

@@ -93,8 +93,9 @@ def tile_tce_kernel(tc, x, adj_t, para, base, offs, out):
         for h in range(PIECES):
             sgn.append(ring.tile([P, PIECE], F32, name="sgn", tag="scalar_out"))
             nc.scalar.activation(sgn[h][:], para_sb[1][:, cols(h)], FUNC.Sign)
+        mag = [ring.tile([P, N], F32, name="mag", tag="scalar_out") for c in range(BLOCKS)]
 
-        rectified, mag = {}, {}
+        rectified = [held.tile([P, N], F32, name=f"rectified{c}") for c in range(BLOCKS)]
         for c in range(BLOCKS):
             for h in range(PIECES):
                 y = psum_y.tile([P, PIECE], F32, name="y")
@@ -109,17 +110,16 @@ def tile_tce_kernel(tc, x, adj_t, para, base, offs, out):
                     )
                 else:
                     nc.vector.tensor_tensor(signed[:], y[:], sgn[h][:], ALU.mult)
-                rectified[c, h] = pieces.tile([P, PIECE], F32, name="rectified")
-                nc.scalar.activation(rectified[c, h][:], signed[:], FUNC.Relu)
-                mag[c, h] = ring.tile([P, PIECE], F32, name="mag", tag="scalar_out")
-                nc.scalar.activation(mag[c, h][:], para_sb[c][:, cols(h)], FUNC.Abs)
+                nc.scalar.activation(rectified[c][:, cols(h)], signed[:], FUNC.Relu)
+                nc.scalar.activation(mag[c][:, cols(h)], para_sb[c][:, cols(h)], FUNC.Abs)
 
         for c in range(BLOCKS):
-            for h in range(PIECES):
+            step = PIECE if c == 0 else N
+            for first in range(0, N, step):
                 nc.vector.tensor_tensor(
-                    window[c][:].indirect(offsets[:, h * (PIECE // 16) : (h + 1) * (PIECE // 16)]),
-                    rectified[c, h][:],
-                    mag[c, h][:],
+                    window[c][:].indirect(offsets[:, first // 16 : (first + step) // 16]),
+                    rectified[c][:, first : first + step],
+                    mag[c][:, first : first + step],
                     ALU.mult,
                 )
             for q in range(STORES):

@@ -95,7 +95,7 @@ def tile_tce_kernel(tc, x, adj_t, para, base, offs, out):
             nc.scalar.activation(sgn[h][:], para_sb[1][:, cols(h)], FUNC.Sign)
         mag = [ring.tile([P, N], F32, name="mag", tag="scalar_out") for c in range(BLOCKS)]
 
-        rectified = [held.tile([P, N], F32, name=f"rectified{c}") for c in range(BLOCKS)]
+        signed = {}
         for c in range(BLOCKS):
             for h in range(PIECES):
                 y = psum_y.tile([P, PIECE], F32, name="y")
@@ -103,25 +103,31 @@ def tile_tce_kernel(tc, x, adj_t, para, base, offs, out):
                     nc.tensor.matmul(
                         y[:], mix[c, k][:], x_sb[:, k, cols(h)], start=(k == 0), stop=(k == BLOCKS - 1)
                     )
-                signed = pieces.tile([P, PIECE], F32, name="signed")
+                signed[c, h] = pieces.tile([P, PIECE], F32, name="signed")
                 if c == 0:
                     nc.vector.scalar_tensor_tensor(
-                        signed[:], twice_pos[:, cols(h)], -1.0, y[:], op0=ALU.add, op1=ALU.mult
+                        signed[c, h][:], twice_pos[:, cols(h)], -1.0, y[:], op0=ALU.add, op1=ALU.mult
                     )
                 else:
-                    nc.vector.tensor_tensor(signed[:], y[:], sgn[h][:], ALU.mult)
-                nc.scalar.activation(rectified[c][:, cols(h)], signed[:], FUNC.Relu)
+                    nc.vector.tensor_tensor(signed[c, h][:], y[:], sgn[h][:], ALU.mult)
+
+        scatters = [(0, 0, 1), (1, 0, PIECES), (0, 1, PIECES - 1)]
+
+        rectified = [held.tile([P, N], F32, name=f"rectified{c}") for c in range(BLOCKS)]
+        for c, first, count in scatters:
+            for h in range(first, first + count):
+                nc.scalar.activation(rectified[c][:, cols(h)], signed[c, h][:], FUNC.Relu)
                 nc.scalar.activation(mag[c][:, cols(h)], para_sb[c][:, cols(h)], FUNC.Abs)
 
-        for c in range(BLOCKS):
-            step = PIECE if c == 0 else N
-            for first in range(0, N, step):
-                nc.vector.tensor_tensor(
-                    window[c][:].indirect(offsets[:, first // 16 : (first + step) // 16]),
-                    rectified[c][:, first : first + step],
-                    mag[c][:, first : first + step],
-                    ALU.mult,
-                )
-            for q in range(STORES):
-                run = slice(q * (S // STORES), (q + 1) * (S // STORES))
-                nc.sync.dma_start(out[c * P : (c + 1) * P, run], window[c][:, run])
+        for c, first, count in scatters:
+            entries = slice(first * PIECE, (first + count) * PIECE)
+            nc.vector.tensor_tensor(
+                window[c][:].indirect(offsets[:, first * (PIECE // 16) : (first + count) * (PIECE // 16)]),
+                rectified[c][:, entries],
+                mag[c][:, entries],
+                ALU.mult,
+            )
+            if first + count == PIECES:
+                for q in range(STORES):
+                    run = slice(q * (S // STORES), (q + 1) * (S // STORES))
+                    nc.sync.dma_start(out[c * P : (c + 1) * P, run], window[c][:, run])

@@ -33,7 +33,7 @@ def tile_tce_kernel(tc, x, adj_t, para, base, offs, out):
         window = [held.tile([P, S], F32, name=f"window{b}") for b in range(BLOCKS)]
 
         nc.sync.dma_start(x_sb[:, 0, :], x[0:P, :])
-        nc.scalar.dma_start(x_sb[:, 1, :], x[P : 2 * P, :])
+        nc.sync.dma_start(x_sb[:, 1, :], x[P : 2 * P, :])
         nc.sync.dma_start(para_sb[0][:], para[0:P, :])
         nc.sync.dma_start(adj_sb[:], adj_t.rearrange("(b p) c -> p b c", p=P))
         nc.sync.dma_start(para_sb[1][:], para[P : 2 * P, :])

@@ -4,12 +4,17 @@ from concourse.masks import make_identity
 P = 128
 C, S, N = 256, 2048, 1024
 BLOCKS = C // P
-PIECE = 512
+BANK = 512
+HALF = N // 2
+PIECE = 256
 PIECES = N // PIECE
+WIDE = 384
+FIRST = 3 * PIECE
 STORES = 4
 FLOPS = 2 * C * C * N
 WARM_UPS = 4
 KEEP_WARM = 2
+BIG = 2.0**64
 
 F32, BF16, U16 = mybir.dt.float32, mybir.dt.bfloat16, mybir.dt.uint16
 FUNC = mybir.ActivationFunctionType
@@ -21,10 +26,9 @@ def tile_tce_kernel(tc, x, adj_t, para, base, offs, out):
     with (
         tc.tile_pool(name="held", bufs=1) as held,
         tc.tile_pool(name="work", bufs=BLOCKS) as work,
-        tc.tile_pool(name="ring", bufs=2 * BLOCKS) as ring,
-        tc.tile_pool(name="pieces", bufs=BLOCKS * PIECES) as pieces,
-        tc.psum_pool(name="psum_row", bufs=1) as psum_row,
-        tc.psum_pool(name="psum_y", bufs=BLOCKS * PIECES) as psum_y,
+        tc.tile_pool(name="ring", bufs=BLOCKS) as ring,
+        tc.tile_pool(name="turns", bufs=1) as turns,
+        tc.psum_pool(name="banks", bufs=8) as banks,
     ):
         offsets = held.tile([P, N // 16], U16, name="offsets")
         x_sb = held.tile([P, BLOCKS, N], BF16, name="x_sb")
@@ -32,21 +36,34 @@ def tile_tce_kernel(tc, x, adj_t, para, base, offs, out):
         para_sb = [held.tile([P, N], F32, name=f"para_sb{b}") for b in range(BLOCKS)]
         window = [held.tile([P, S], F32, name=f"window{b}") for b in range(BLOCKS)]
 
+        pieces0 = [slice(q * PIECE, (q + 1) * PIECE) for q in range(PIECES)]
+        pieces1 = [slice(j, min(j + WIDE, N)) for j in range(0, N, WIDE)]
+
+        def bank():
+            return banks.tile([P, BANK], F32, name="bank")
+
+        low, high = slice(0, HALF), slice(HALF, N)
         nc.sync.dma_start(x_sb[:, 0, :], x[0:P, :])
         nc.sync.dma_start(x_sb[:, 1, :], x[P : 2 * P, :])
-        nc.sync.dma_start(para_sb[0][:], para[0:P, :])
+        nc.sync.dma_start(para_sb[0][:, low], para[0:P, low])
         nc.sync.dma_start(adj_sb[:], adj_t.rearrange("(b p) c -> p b c", p=P))
-        nc.sync.dma_start(para_sb[1][:], para[P : 2 * P, :])
+        nc.sync.dma_start(para_sb[0][:, high], para[0:P, high])
+        nc.sync.dma_start(para_sb[1][:, 0:WIDE], para[P : 2 * P, 0:WIDE])
         nc.sync.dma_start(offsets[:], offs)
         nc.sync.dma_start(window[0][:], base[0:P, :])
+        nc.sync.dma_start(para_sb[1][:, WIDE:N], para[P : 2 * P, WIDE:N])
         nc.sync.dma_start(window[1][:], base[P : 2 * P, :])
 
         identity = held.tile([P, P], F32, name="identity")
         make_identity(nc, identity[:])
+        big_identity = held.tile([P, P], BF16, name="big_identity")
+        nc.gpsimd.tensor_scalar(big_identity[:], identity[:], BIG, None, op0=ALU.mult)
+        minus_big_identity = held.tile([P, P], BF16, name="minus_big_identity")
+        nc.gpsimd.tensor_scalar(minus_big_identity[:], identity[:], -BIG, None, op0=ALU.mult)
 
-        idle_work = psum_row.tile([P, P], F32, name="idle_work")
+        idle_work = bank()
         for i in range(WARM_UPS):
-            nc.tensor.matmul(idle_work[:], identity[:], identity[:], start=True, stop=True)
+            nc.tensor.matmul(idle_work[:, 0:P], identity[:], identity[:], start=True, stop=True)
 
         warm = held.tile([P, 1], F32, name="warm")
         nc.vector.memset(warm[:], 0.0)
@@ -60,74 +77,107 @@ def tile_tce_kernel(tc, x, adj_t, para, base, offs, out):
                 copied[:], x_sb[:, b, :], 1.0, None, op0=ALU.mult, op1=ALU.add, accum_out=rowsum[b][:]
             )
 
-        sums_row = [psum_row.tile([P, P], F32, name=f"sums_row{b}") for b in range(BLOCKS)]
+        sums_row = [bank() for b in range(BLOCKS)]
         for b in range(BLOCKS):
-            nc.tensor.transpose(sums_row[b][:], rowsum[b][:, 0:1].to_broadcast([P, P]), identity[:])
+            nc.tensor.transpose(sums_row[b][:, 0:P], rowsum[b][:, 0:1].to_broadcast([P, P]), identity[:])
 
         for i in range(KEEP_WARM):
             nc.tensor.matmul(
-                idle_work[:], identity[:], rowsum[BLOCKS - 1][:, 0:1].to_broadcast([P, P]), start=True, stop=True
+                idle_work[:, 0:P], identity[:], rowsum[BLOCKS - 1][:, 0:1].to_broadcast([P, P]), start=True, stop=True
             )
 
-        def cols(h):
-            return slice(h * PIECE, (h + 1) * PIECE)
+        def twice_positive(twice_pos, columns):
+            nc.vector.tensor_scalar(twice_pos[:], para_sb[0][:, columns], 0.0, 2.0, op0=ALU.is_ge, op1=ALU.mult)
+            return twice_pos
 
-        twice_pos = held.tile([P, N], F32, name="twice_pos")
-        nc.vector.tensor_scalar(twice_pos[:], para_sb[0][:], 0.0, 2.0, op0=ALU.is_ge, op1=ALU.mult)
+        signs = [twice_positive(held.tile([P, PIECE], F32, name=f"twice_pos{q}"), pieces0[q]) for q in range(2)]
+        signs.append(twice_positive(turns.tile([P, PIECE], F32, name="twice_pos2"), pieces0[2]))
 
-        mix = {}
-        for c in range(BLOCKS):
+        def half_of_s(c):
             gap = [work.tile([P, P], F32, name="gap") for k in range(BLOCKS)]
             for k in range(BLOCKS):
-                nc.scalar.activation(gap[k][:], sums_row[c][:], FUNC.Abs, bias=rowsum[k][:, 0:1], scale=-1.0)
-            half_s = [ring.tile([P, P], F32, name="half_s", tag="scalar_out") for k in range(BLOCKS)]
+                nc.scalar.activation(gap[k][:], sums_row[c][:, 0:P], FUNC.Abs, bias=rowsum[k][:, 0:1], scale=-1.0)
+            half_s = [ring.tile([P, P], F32, name="half_s", tag=f"half_s{c}") for k in range(BLOCKS)]
             for k in range(BLOCKS):
                 nc.scalar.activation(half_s[k][:], gap[k][:], FUNC.Sigmoid, scale=-1.0 / N)
+            return half_s
+
+        def weights(c, half_s):
+            mix = turns.tile([P, BLOCKS, P], BF16, name=f"mix{c}", tag=["mix0", "twice_pos2"][c])
             for k in range(BLOCKS):
-                mix[c, k] = held.tile([P, P], BF16, name=f"mix{c}{k}")
                 nc.vector.scalar_tensor_tensor(
-                    mix[c, k][:], half_s[k][:], 2.0, adj_sb[:, k, c * P : (c + 1) * P], op0=ALU.mult, op1=ALU.mult
+                    mix[:, k, :], half_s[k][:], 2.0, adj_sb[:, k, c * P : (c + 1) * P], op0=ALU.mult, op1=ALU.mult
+                )
+            return mix
+
+        mix = [weights(0, half_of_s(0))]
+        half_s1 = half_of_s(1)
+
+        signs.append(twice_positive(ring.tile([P, PIECE], F32, name="twice_pos3", tag="half_s0"), pieces0[3]))
+        mag0 = ring.tile([P, FIRST], F32, name="mag0", tag="half_s0")
+        nc.scalar.activation(mag0[:], para_sb[0][:, 0:FIRST], FUNC.Abs)
+
+        def products(y, c, columns, stop):
+            for k in range(BLOCKS):
+                nc.tensor.matmul(
+                    y, mix[c][:, k, :], x_sb[:, k, columns], start=(k == 0), stop=(stop and k == BLOCKS - 1)
                 )
 
-        sgn = []
-        for h in range(PIECES):
-            sgn.append(ring.tile([P, PIECE], F32, name="sgn", tag="scalar_out"))
-            nc.scalar.activation(sgn[h][:], para_sb[1][:, cols(h)], FUNC.Sign)
-        mag = [ring.tile([P, N], F32, name="mag", tag="scalar_out") for c in range(BLOCKS)]
-
-        signed = {}
-        for c in range(BLOCKS):
-            for h in range(PIECES):
-                y = psum_y.tile([P, PIECE], F32, name="y")
-                for k in range(BLOCKS):
-                    nc.tensor.matmul(
-                        y[:], mix[c, k][:], x_sb[:, k, cols(h)], start=(k == 0), stop=(k == BLOCKS - 1)
-                    )
-                signed[c, h] = pieces.tile([P, PIECE], F32, name="signed")
-                if c == 0:
-                    nc.vector.scalar_tensor_tensor(
-                        signed[c, h][:], twice_pos[:, cols(h)], -1.0, y[:], op0=ALU.add, op1=ALU.mult
-                    )
-                else:
-                    nc.vector.tensor_tensor(signed[c, h][:], y[:], sgn[h][:], ALU.mult)
-
-        scatters = [(0, 0, 1), (1, 0, PIECES), (0, 1, PIECES - 1)]
-
         rectified = [held.tile([P, N], F32, name=f"rectified{c}") for c in range(BLOCKS)]
-        for c, first, count in scatters:
-            for h in range(first, first + count):
-                nc.scalar.activation(rectified[c][:, cols(h)], signed[c, h][:], FUNC.Relu)
-                nc.scalar.activation(mag[c][:, cols(h)], para_sb[c][:, cols(h)], FUNC.Abs)
 
-        for c, first, count in scatters:
-            entries = slice(first * PIECE, (first + count) * PIECE)
+        for q in range(PIECES):
+            y = bank()
+            products(y[:, 0:PIECE], 0, pieces0[q], stop=True)
+            signed = turns.tile([P, PIECE], F32, name="signed", tag=f"signed{q}")
+            nc.vector.scalar_tensor_tensor(
+                signed[:], signs[q][:], -1.0, y[:, 0:PIECE], op0=ALU.add, op1=ALU.mult
+            )
+            nc.scalar.activation(rectified[0][:, pieces0[q]], signed[:], FUNC.Relu)
+            if (q + 1) * PIECE == FIRST:
+                mix.append(weights(1, half_s1))
+
+        mag1 = ring.tile([P, N], F32, name="mag1", tag="half_s1")
+        masked = []
+        for i in range(len(pieces1) + 1):
+            if i < len(pieces1):
+                columns = pieces1[i]
+                width = columns.stop - columns.start
+                sieve = turns.tile([P, 2, WIDE], BF16, name="sieve", tag=f"signed{PIECES - 2 + i % 2}")
+                masked.append([turns.tile([P, WIDE], F32, name=f"masked{i}{side}") for side in range(2)])
+                for side, flip in enumerate((-1.0, 1.0)):
+                    nc.scalar.activation(sieve[:, side, 0:width], para_sb[1][:, columns], FUNC.Relu, scale=flip)
+                for side, (flip, weight) in enumerate(((1.0, minus_big_identity), (-1.0, big_identity))):
+                    y = bank()
+                    products(y[:, 0:width], 1, columns, stop=False)
+                    nc.tensor.matmul(y[:, 0:width], weight[:], sieve[:, side, 0:width], start=False, stop=True)
+                    nc.scalar.activation(masked[i][side][:, 0:width], y[:, 0:width], FUNC.Relu, scale=flip)
+                nc.scalar.activation(mag1[:, columns], para_sb[1][:, columns], FUNC.Abs)
+            if i > 0:
+                columns = pieces1[i - 1]
+                width = columns.stop - columns.start
+                both = bank()
+                for side in range(2):
+                    nc.tensor.matmul(
+                        both[:, 0:width], identity[:], masked[i - 1][side][:, 0:width], start=(side == 0), stop=(side == 1)
+                    )
+                nc.scalar.activation(rectified[1][:, columns], both[:, 0:width], FUNC.Copy)
+            if i == 1:
+                mag0_rest = turns.tile([P, N - FIRST], F32, name="mag0_rest", tag="masked01")
+                nc.scalar.activation(mag0_rest[:], para_sb[0][:, FIRST:N], FUNC.Abs)
+
+        for c, first, end, magnitude in [
+            (0, 0, FIRST, mag0[:]),
+            (1, 0, WIDE, mag1[:, 0:WIDE]),
+            (0, FIRST, N, mag0_rest[:]),
+            (1, WIDE, N, mag1[:, WIDE:N]),
+        ]:
             nc.vector.tensor_tensor(
-                window[c][:].indirect(offsets[:, first * (PIECE // 16) : (first + count) * (PIECE // 16)]),
-                rectified[c][:, entries],
-                mag[c][:, entries],
+                window[c][:].indirect(offsets[:, first // 16 : end // 16]),
+                rectified[c][:, first:end],
+                magnitude,
                 ALU.mult,
             )
-            if first + count == PIECES:
+            if end == N:
                 for q in range(STORES):
                     run = slice(q * (S // STORES), (q + 1) * (S // STORES))
                     nc.sync.dma_start(out[c * P : (c + 1) * P, run], window[c][:, run])

@@ -48,9 +48,9 @@ def tile_tce_kernel(tc, x, adj_t, para, base, offs, out):
         nc.sync.dma_start(para_sb[0][:, low], para[0:P, low])
         nc.sync.dma_start(adj_sb[:], adj_t.rearrange("(b p) c -> p b c", p=P))
         nc.sync.dma_start(para_sb[0][:, high], para[0:P, high])
-        nc.sync.dma_start(para_sb[1][:, 0:WIDE], para[P : 2 * P, 0:WIDE])
         nc.sync.dma_start(offsets[:], offs)
         nc.sync.dma_start(window[0][:], base[0:P, :])
+        nc.sync.dma_start(para_sb[1][:, 0:WIDE], para[P : 2 * P, 0:WIDE])
         nc.sync.dma_start(para_sb[1][:, WIDE:N], para[P : 2 * P, WIDE:N])
         nc.sync.dma_start(window[1][:], base[P : 2 * P, :])
 
@@ -90,8 +90,7 @@ def tile_tce_kernel(tc, x, adj_t, para, base, offs, out):
             nc.vector.tensor_scalar(twice_pos[:], para_sb[0][:, columns], 0.0, 2.0, op0=ALU.is_ge, op1=ALU.mult)
             return twice_pos
 
-        signs = [twice_positive(held.tile([P, PIECE], F32, name=f"twice_pos{q}"), pieces0[q]) for q in range(2)]
-        signs.append(twice_positive(turns.tile([P, PIECE], F32, name="twice_pos2"), pieces0[2]))
+        signs = [twice_positive(held.tile([P, PIECE], F32, name=f"twice_pos{q}"), pieces0[q]) for q in range(3)]
 
         def half_of_s(c):
             gap = [work.tile([P, P], F32, name="gap") for k in range(BLOCKS)]
@@ -102,16 +101,15 @@ def tile_tce_kernel(tc, x, adj_t, para, base, offs, out):
                 nc.scalar.activation(half_s[k][:], gap[k][:], FUNC.Sigmoid, scale=-1.0 / N)
             return half_s
 
-        def weights(c, half_s):
-            mix = turns.tile([P, BLOCKS, P], BF16, name=f"mix{c}", tag=["mix0", "twice_pos2"][c])
-            for k in range(BLOCKS):
-                nc.vector.scalar_tensor_tensor(
-                    mix[:, k, :], half_s[k][:], 2.0, adj_sb[:, k, c * P : (c + 1) * P], op0=ALU.mult, op1=ALU.mult
-                )
-            return mix
-
-        mix = [weights(0, half_of_s(0))]
+        mix = [held.tile([P, BLOCKS, P], BF16, name=f"mix{c}") for c in range(BLOCKS)]
+        half_s0 = half_of_s(0)
+        for k in range(BLOCKS):
+            nc.vector.scalar_tensor_tensor(
+                mix[0][:, k, :], half_s0[k][:], 2.0, adj_sb[:, k, 0:P], op0=ALU.mult, op1=ALU.mult
+            )
         half_s1 = half_of_s(1)
+        for k in range(BLOCKS):
+            nc.gpsimd.tensor_tensor(mix[1][:, k, :], half_s1[k][:], adj_sb[:, k, P:C], ALU.mult)
 
         signs.append(twice_positive(ring.tile([P, PIECE], F32, name="twice_pos3", tag="half_s0"), pieces0[3]))
         mag0 = ring.tile([P, FIRST], F32, name="mag0", tag="half_s0")
@@ -133,8 +131,6 @@ def tile_tce_kernel(tc, x, adj_t, para, base, offs, out):
                 signed[:], signs[q][:], -1.0, y[:, 0:PIECE], op0=ALU.add, op1=ALU.mult
             )
             nc.scalar.activation(rectified[0][:, pieces0[q]], signed[:], FUNC.Relu)
-            if (q + 1) * PIECE == FIRST:
-                mix.append(weights(1, half_s1))
 
         mag1 = ring.tile([P, N], F32, name="mag1", tag="half_s1")
         masked = []
@@ -150,7 +146,7 @@ def tile_tce_kernel(tc, x, adj_t, para, base, offs, out):
                     y = bank()
                     products(y[:, 0:width], 1, columns, stop=False)
                     nc.tensor.matmul(y[:, 0:width], weight[:], sieve[:, side, 0:width], start=False, stop=True)
-                    nc.scalar.activation(masked[i][side][:, 0:width], y[:, 0:width], FUNC.Relu, scale=flip)
+                    nc.scalar.activation(masked[i][side][:, 0:width], y[:, 0:width], FUNC.Relu, scale=2.0 * flip)
                 nc.scalar.activation(mag1[:, columns], para_sb[1][:, columns], FUNC.Abs)
             if i > 0:
                 columns = pieces1[i - 1]

@@ -162,7 +162,8 @@ def tile_tce_kernel(tc, x, adj_t, para, base, offs, out):
                 nc.scalar.activation(mag0_rest[:], para_sb[0][:, FIRST:N], FUNC.Abs)
 
         for c, first, end, magnitude in [
-            (0, 0, FIRST, mag0[:]),
+            (0, 0, PIECE, mag0[:, 0:PIECE]),
+            (0, PIECE, FIRST, mag0[:, PIECE:FIRST]),
             (1, 0, WIDE, mag1[:, 0:WIDE]),
             (0, FIRST, N, mag0_rest[:]),
             (1, WIDE, N, mag1[:, WIDE:N]),

@@ -10,7 +10,7 @@ PIECE = 256
 PIECES = N // PIECE
 WIDE = 384
 FIRST = 3 * PIECE
-STORES = 4
+STORES = 2
 FLOPS = 2 * C * C * N
 WARM_UPS = 4
 KEEP_WARM = 2

@@ -5,12 +5,11 @@ P = 128
 C, S, N = 256, 2048, 1024
 BLOCKS = C // P
 BANK = 512
-HALF = N // 2
 PIECE = 256
 PIECES = N // PIECE
 WIDE = 384
 FIRST = 3 * PIECE
-STORES = 2
+STORES = (1, 2)
 FLOPS = 2 * C * C * N
 WARM_UPS = 4
 KEEP_WARM = 2
@@ -42,12 +41,10 @@ def tile_tce_kernel(tc, x, adj_t, para, base, offs, out):
         def bank():
             return banks.tile([P, BANK], F32, name="bank")
 
-        low, high = slice(0, HALF), slice(HALF, N)
         nc.sync.dma_start(x_sb[:, 0, :], x[0:P, :])
         nc.sync.dma_start(x_sb[:, 1, :], x[P : 2 * P, :])
-        nc.sync.dma_start(para_sb[0][:, low], para[0:P, low])
+        nc.sync.dma_start(para_sb[0][:], para[0:P, :])
         nc.sync.dma_start(adj_sb[:], adj_t.rearrange("(b p) c -> p b c", p=P))
-        nc.sync.dma_start(para_sb[0][:, high], para[0:P, high])
         nc.sync.dma_start(offsets[:], offs)
         nc.sync.dma_start(window[0][:], base[0:P, :])
         nc.sync.dma_start(para_sb[1][:, 0:WIDE], para[P : 2 * P, 0:WIDE])
@@ -175,6 +172,6 @@ def tile_tce_kernel(tc, x, adj_t, para, base, offs, out):
                 ALU.mult,
             )
             if end == N:
-                for q in range(STORES):
-                    run = slice(q * (S // STORES), (q + 1) * (S // STORES))
-                    nc.sync.dma_start(out[c * P : (c + 1) * P, run], window[c][:, run])
+                width = S // STORES[c]
+                for j in range(0, S, width):
+                    nc.sync.dma_start(out[c * P : (c + 1) * P, j : j + width], window[c][:, j : j + width])

@@ -9,7 +9,7 @@ PIECE = 256
 PIECES = N // PIECE
 WIDE = 384
 FIRST = 3 * PIECE
-STORES = (1, 2)
+STORES = (4, 2)
 FLOPS = 2 * C * C * N
 WARM_UPS = 4
 KEEP_WARM = 2

@@ -159,8 +159,7 @@ def tile_tce_kernel(tc, x, adj_t, para, base, offs, out):
                 nc.scalar.activation(mag0_rest[:], para_sb[0][:, FIRST:N], FUNC.Abs)
 
         for c, first, end, magnitude in [
-            (0, 0, PIECE, mag0[:, 0:PIECE]),
-            (0, PIECE, FIRST, mag0[:, PIECE:FIRST]),
+            (0, 0, FIRST, mag0[:]),
             (1, 0, WIDE, mag1[:, 0:WIDE]),
             (0, FIRST, N, mag0_rest[:]),
             (1, WIDE, N, mag1[:, WIDE:N]),

import concourse.mybir as mybir
from concourse.masks import make_identity

P = 128
C, S, N = 256, 2048, 1024
BLOCKS = C // P
BANK = 512
PIECE = 256
PIECES = N // PIECE
WIDE = 384
FIRST = 3 * PIECE
STORES = (4, 2)
FLOPS = 2 * C * C * N
WARM_UPS = 4
KEEP_WARM = 2
BIG = 2.0**64

F32, BF16, U16 = mybir.dt.float32, mybir.dt.bfloat16, mybir.dt.uint16
FUNC = mybir.ActivationFunctionType
ALU = mybir.AluOpType


def tile_tce_kernel(tc, x, adj_t, para, base, offs, out):
    nc = tc.nc
    with (
        tc.tile_pool(name="held", bufs=1) as held,
        tc.tile_pool(name="work", bufs=BLOCKS) as work,
        tc.tile_pool(name="ring", bufs=BLOCKS) as ring,
        tc.tile_pool(name="turns", bufs=1) as turns,
        tc.psum_pool(name="banks", bufs=8) as banks,
    ):
        offsets = held.tile([P, N // 16], U16, name="offsets")
        x_sb = held.tile([P, BLOCKS, N], BF16, name="x_sb")
        adj_sb = held.tile([P, BLOCKS, C], F32, name="adj_sb")
        para_sb = [held.tile([P, N], F32, name=f"para_sb{b}") for b in range(BLOCKS)]
        window = [held.tile([P, S], F32, name=f"window{b}") for b in range(BLOCKS)]

        pieces0 = [slice(q * PIECE, (q + 1) * PIECE) for q in range(PIECES)]
        pieces1 = [slice(j, min(j + WIDE, N)) for j in range(0, N, WIDE)]

        def bank():
            return banks.tile([P, BANK], F32, name="bank")

        nc.sync.dma_start(x_sb[:, 0, :], x[0:P, :])
        nc.sync.dma_start(x_sb[:, 1, :], x[P : 2 * P, :])
        nc.sync.dma_start(para_sb[0][:], para[0:P, :])
        nc.sync.dma_start(adj_sb[:], adj_t.rearrange("(b p) c -> p b c", p=P))
        nc.sync.dma_start(offsets[:], offs)
        nc.sync.dma_start(window[0][:], base[0:P, :])
        nc.sync.dma_start(para_sb[1][:, 0:WIDE], para[P : 2 * P, 0:WIDE])
        nc.sync.dma_start(para_sb[1][:, WIDE:N], para[P : 2 * P, WIDE:N])
        nc.sync.dma_start(window[1][:], base[P : 2 * P, :])

        identity = held.tile([P, P], F32, name="identity")
        make_identity(nc, identity[:])
        big_identity = held.tile([P, P], BF16, name="big_identity")
        nc.gpsimd.tensor_scalar(big_identity[:], identity[:], BIG, None, op0=ALU.mult)
        minus_big_identity = held.tile([P, P], BF16, name="minus_big_identity")
        nc.gpsimd.tensor_scalar(minus_big_identity[:], identity[:], -BIG, None, op0=ALU.mult)

        idle_work = bank()
        for i in range(WARM_UPS):
            nc.tensor.matmul(idle_work[:, 0:P], identity[:], identity[:], start=True, stop=True)

        warm = held.tile([P, 1], F32, name="warm")
        nc.vector.memset(warm[:], 0.0)
        warmed = held.tile([P, 1], F32, name="warmed")
        nc.scalar.activation(warmed[:], warm[:], FUNC.Sigmoid)

        rowsum = [held.tile([P, 1], F32, name=f"rowsum{b}") for b in range(BLOCKS)]
        for b in range(BLOCKS):
            copied = work.tile([P, N], BF16, name="copied")
            nc.vector.tensor_scalar(
                copied[:], x_sb[:, b, :], 1.0, None, op0=ALU.mult, op1=ALU.add, accum_out=rowsum[b][:]
            )

        sums_row = [bank() for b in range(BLOCKS)]
        for b in range(BLOCKS):
            nc.tensor.transpose(sums_row[b][:, 0:P], rowsum[b][:, 0:1].to_broadcast([P, P]), identity[:])

        for i in range(KEEP_WARM):
            nc.tensor.matmul(
                idle_work[:, 0:P], identity[:], rowsum[BLOCKS - 1][:, 0:1].to_broadcast([P, P]), start=True, stop=True
            )

        def twice_positive(twice_pos, columns):
            nc.vector.tensor_scalar(twice_pos[:], para_sb[0][:, columns], 0.0, 2.0, op0=ALU.is_ge, op1=ALU.mult)
            return twice_pos

        signs = [twice_positive(held.tile([P, PIECE], F32, name=f"twice_pos{q}"), pieces0[q]) for q in range(3)]

        def half_of_s(c):
            gap = [work.tile([P, P], F32, name="gap") for k in range(BLOCKS)]
            for k in range(BLOCKS):
                nc.scalar.activation(gap[k][:], sums_row[c][:, 0:P], FUNC.Abs, bias=rowsum[k][:, 0:1], scale=-1.0)
            half_s = [ring.tile([P, P], F32, name="half_s", tag=f"half_s{c}") for k in range(BLOCKS)]
            for k in range(BLOCKS):
                nc.scalar.activation(half_s[k][:], gap[k][:], FUNC.Sigmoid, scale=-1.0 / N)
            return half_s

        mix = [held.tile([P, BLOCKS, P], BF16, name=f"mix{c}") for c in range(BLOCKS)]
        half_s0 = half_of_s(0)
        for k in range(BLOCKS):
            nc.vector.scalar_tensor_tensor(
                mix[0][:, k, :], half_s0[k][:], 2.0, adj_sb[:, k, 0:P], op0=ALU.mult, op1=ALU.mult
            )
        half_s1 = half_of_s(1)
        for k in range(BLOCKS):
            nc.gpsimd.tensor_tensor(mix[1][:, k, :], half_s1[k][:], adj_sb[:, k, P:C], ALU.mult)

        signs.append(twice_positive(ring.tile([P, PIECE], F32, name="twice_pos3", tag="half_s0"), pieces0[3]))
        mag0 = ring.tile([P, FIRST], F32, name="mag0", tag="half_s0")
        nc.scalar.activation(mag0[:], para_sb[0][:, 0:FIRST], FUNC.Abs)

        def products(y, c, columns, stop):
            for k in range(BLOCKS):
                nc.tensor.matmul(
                    y, mix[c][:, k, :], x_sb[:, k, columns], start=(k == 0), stop=(stop and k == BLOCKS - 1)
                )

        rectified = [held.tile([P, N], F32, name=f"rectified{c}") for c in range(BLOCKS)]

        for q in range(PIECES):
            y = bank()
            products(y[:, 0:PIECE], 0, pieces0[q], stop=True)
            signed = turns.tile([P, PIECE], F32, name="signed", tag=f"signed{q}")
            nc.vector.scalar_tensor_tensor(
                signed[:], signs[q][:], -1.0, y[:, 0:PIECE], op0=ALU.add, op1=ALU.mult
            )
            nc.scalar.activation(rectified[0][:, pieces0[q]], signed[:], FUNC.Relu)

        mag1 = ring.tile([P, N], F32, name="mag1", tag="half_s1")
        masked = []
        for i in range(len(pieces1) + 1):
            if i < len(pieces1):
                columns = pieces1[i]
                width = columns.stop - columns.start
                sieve = turns.tile([P, 2, WIDE], BF16, name="sieve", tag=f"signed{PIECES - 2 + i % 2}")
                masked.append([turns.tile([P, WIDE], F32, name=f"masked{i}{side}") for side in range(2)])
                for side, flip in enumerate((-1.0, 1.0)):
                    nc.scalar.activation(sieve[:, side, 0:width], para_sb[1][:, columns], FUNC.Relu, scale=flip)
                for side, (flip, weight) in enumerate(((1.0, minus_big_identity), (-1.0, big_identity))):
                    y = bank()
                    products(y[:, 0:width], 1, columns, stop=False)
                    nc.tensor.matmul(y[:, 0:width], weight[:], sieve[:, side, 0:width], start=False, stop=True)
                    nc.scalar.activation(masked[i][side][:, 0:width], y[:, 0:width], FUNC.Relu, scale=2.0 * flip)
                nc.scalar.activation(mag1[:, columns], para_sb[1][:, columns], FUNC.Abs)
            if i > 0:
                columns = pieces1[i - 1]
                width = columns.stop - columns.start
                both = bank()
                for side in range(2):
                    nc.tensor.matmul(
                        both[:, 0:width], identity[:], masked[i - 1][side][:, 0:width], start=(side == 0), stop=(side == 1)
                    )
                nc.scalar.activation(rectified[1][:, columns], both[:, 0:width], FUNC.Copy)
            if i == 1:
                mag0_rest = turns.tile([P, N - FIRST], F32, name="mag0_rest", tag="masked01")
                nc.scalar.activation(mag0_rest[:], para_sb[0][:, FIRST:N], FUNC.Abs)

        for c, first, end, magnitude in [
            (0, 0, FIRST, mag0[:]),
            (1, 0, WIDE, mag1[:, 0:WIDE]),
            (0, FIRST, N, mag0_rest[:]),
            (1, WIDE, N, mag1[:, WIDE:N]),
        ]:
            nc.vector.tensor_tensor(
                window[c][:].indirect(offsets[:, first // 16 : end // 16]),
                rectified[c][:, first:end],
                magnitude,
                ALU.mult,
            )
            if end == N:
                width = S // STORES[c]
                for j in range(0, S, width):
                    nc.sync.dma_start(out[c * P : (c + 1) * P, j : j + width], window[c][:, j : j + width])
